import numpy as np
import ml_dtypes


def mxq(x, axis, fmt="e4m3"):
    dtype, down = {"e4m3": (ml_dtypes.float8_e4m3fn, 7), "e5m2": (ml_dtypes.float8_e5m2, 14)}[fmt]
    v = np.moveaxis(np.asarray(x, np.float32).astype(ml_dtypes.bfloat16).astype(np.float64), axis, -1)
    blocks = v.reshape(v.shape[:-1] + (-1, 32))
    amax = np.abs(blocks).max(-1, keepdims=True)
    byte = np.maximum(np.where(amax > 0, np.frexp(amax)[1] - 1 + 127, 0) - down, 1)
    scale = np.exp2(byte - 127.0)
    codes = (blocks / scale).astype(np.float32).astype(dtype).astype(np.float64)
    return np.moveaxis((codes * scale).reshape(v.shape), -1, axis)


WIDE = False


def mx_kscale(k):
    if not WIDE:
        return np.ones(k)
    levels = np.array([10, -10, 5, -5, 0])
    a = np.random.permutation(np.resize(levels, k // 512 * 4)).reshape(k // 512, 4)
    idx = np.arange(k)
    return np.exp2(a[idx // 512, idx % 128 // 32])


BF16 = ml_dtypes.bfloat16


def bf(x):
    return np.asarray(x, np.float32).astype(BF16)


def f64(x):
    return np.asarray(x).astype(np.float64)


N, K, F, NB = 4096, 512, 128, 32


def setup_inputs():
    s = mx_kscale(N)
    c = s / s.min()
    r = s.max() / s
    edge = np.random.random_sample((N, N)) < NB / N
    return {"h_ln": bf(np.random.standard_normal((N, F)) * r[:, None]),
            "adj": bf(np.random.random_sample((N, N)) * edge * c[None, :]),
            "W2": bf(np.random.standard_normal((F, F)) * 2.0 / np.sqrt(F)),
            "b2": bf(np.random.standard_normal(F) * 0.2)}


def reference(h_ln, adj, W2, b2):
    a = f64(adj)
    h = f64(h_ln) @ f64(W2) + f64(b2)
    deg = a.sum(axis=1) + 1.0
    dinv = np.where(deg > 0, deg ** -0.5, 0.0)
    hs = dinv[:, None] * h
    agg = (mxq(a, 1, "e4m3") @ mxq(hs, 0, "e4m3")) + hs
    return dinv[:, None] * agg

@@ -1,0 +1,210 @@
+import concourse.mybir as mybir
+from concourse.masks import make_identity
+
+F32 = mybir.dt.float32
+BF16 = mybir.dt.bfloat16
+U32 = mybir.dt.uint32
+U8 = mybir.dt.uint8
+FP8X4 = mybir.dt.float8_e4m3fn_x4
+ALU = mybir.AluOpType
+ACT = mybir.ActivationFunctionType
+
+P = 128
+NODES = 4096
+FEATS = 128
+TILES = NODES // P
+PACK = 4
+K_PASS = P * PACK
+PASSES = NODES // K_PASS
+BANK = 512
+PASSES_IN_BANK = BANK // (2 * P)
+BANKS_IN_TILE = PASSES // PASSES_IN_BANK
+TILES_IN_BANK = BANK // FEATS
+FEATURE_GROUP = 8
+
+SCALAR_SUM_COLS = 768
+VECTOR_SUM_COLS = NODES - SCALAR_SUM_COLS
+
+SMALLEST_DEG = 2.0**-100
+
+FLOPS = 2 * NODES * NODES * FEATS + 2 * NODES * FEATS * FEATS
+
+
+def tile_gcnlayer_pb_t_kernel(tc, h_ln, adj, W2, b2, out):
+    nc = tc.nc
+
+    adj_tiles = adj.rearrange("(g p e) j -> p g e j", p=P, e=2)
+    h_ln_spans = h_ln.rearrange("(g p e) k -> p g (e k)", p=P, e=2)
+    out_spans = out.rearrange("(g p e) f -> p g (e f)", p=P, e=2)
+
+    with tc.tile_pool(name="keep", bufs=1) as keep, tc.psum_pool(name="psum", bufs=8) as psum:
+        ident_f32 = keep.tile([P, P], F32)
+        make_identity(nc, ident_f32[:])
+        ident_bf16 = keep.tile([P, P], BF16)
+        make_identity(nc, ident_bf16[:])
+        w2_sb = keep.tile([FEATS, FEATS], BF16)
+        nc.scalar.dma_start(out=w2_sb[:], in_=W2)
+        ones = keep.tile([P, P], BF16)
+        nc.vector.memset(ones[:], 1.0)
+        bias_rows = keep.tile([P, FEATS], BF16)
+        nc.vector.memset(bias_rows[:], 0.0)
+        nc.scalar.dma_start(out=bias_rows[0:1, :], in_=b2.rearrange("(o f) -> o f", o=1))
+        table_warmer = keep.tile([P, 1], F32)
+        nc.vector.memset(table_warmer[:], 1.0)
+        nc.scalar.activation(out=table_warmer[:], in_=table_warmer[:], func=ACT.Sqrt)
+
+        adj_codes = keep.tile([P, TILES, PASSES * P], U32, align_bytes=64)
+        adj_scales = keep.tile([P, TILES, PASSES * P], U8, align_bytes=64)
+        h_lnT = keep.tile([FEATS, NODES], BF16)
+        sums_vector = keep.tile([P, TILES], F32)
+        sums_scalar = keep.tile([P, TILES], F32)
+
+        with tc.tile_pool(name="stream", bufs=1) as stream:
+            unread_vector = stream.tile([P, VECTOR_SUM_COLS], BF16)
+            unread_scalar = stream.tile([P, SCALAR_SUM_COLS], BF16)
+            turned = {}
+            for s in range(TILES + 1):
+                if s < TILES:
+                    rows = stream.tile([P, NODES], BF16, tag="rows", bufs=4)
+                    nc.sync.dma_start(out=rows[:], in_=adj_tiles[:, s // 2, s % 2, :])
+
+                    nc.vector.tensor_scalar(
+                        out=unread_vector[:],
+                        in0=rows[:, :VECTOR_SUM_COLS],
+                        scalar1=1.0,
+                        scalar2=None,
+                        op0=ALU.mult,
+                        op1=ALU.add,
+                        accum_out=sums_vector[:, s : s + 1],
+                    )
+                    nc.scalar.activation(
+                        out=unread_scalar[:],
+                        in_=rows[:, VECTOR_SUM_COLS:],
+                        func=ACT.Copy,
+                        accum_out=sums_scalar[:, s : s + 1],
+                    )
+
+                    place = s % FEATURE_GROUP
+                    if place == 0:
+                        features = stream.tile([P, FEATURE_GROUP * FEATS], BF16, tag="features", bufs=2)
+                        first_span = s // 2
+                        nc.sync.dma_start(
+                            out=features[:].rearrange("p (g x) -> p g x", x=2 * FEATS),
+                            in_=h_ln_spans[:, first_span : first_span + FEATURE_GROUP // 2, :],
+                        )
+                        features_bank = psum.tile([FEATS, FEATURE_GROUP * P], BF16, tag="bank")
+                    nc.tensor.transpose(
+                        features_bank[:, place * P : (place + 1) * P],
+                        features[:, place * FEATS : (place + 1) * FEATS],
+                        ident_bf16[:],
+                    )
+                    if place == FEATURE_GROUP - 1:
+                        nc.scalar.copy(
+                            out=h_lnT[:, (s - place) * P : (s + 1) * P], in_=features_bank[:]
+                        )
+
+                    row_words = rows[:].bitcast(F32)
+                    grouped = stream.tile([P, NODES], BF16, tag="grouped", bufs=2, align_bytes=64)
+                    grouped_words = grouped[:].bitcast(F32).rearrange(
+                        "q (c i u) -> q c i u", c=PASSES, u=2
+                    )
+                    for b in range(BANKS_IN_TILE):
+                        bank = psum.tile([P, BANK], F32, tag="bank")
+                        for half in range(2 * PASSES_IN_BANK):
+                            block = 2 * PASSES_IN_BANK * b + half
+                            nc.tensor.transpose(
+                                bank[:, half * P : (half + 1) * P],
+                                row_words[:, block * P : (block + 1) * P],
+                                ident_f32[:],
+                            )
+                        nc.scalar.copy(
+                            out=grouped_words[:, b * PASSES_IN_BANK : (b + 1) * PASSES_IN_BANK, :, :],
+                            in_=bank[:].rearrange("q (c u i) -> q c i u", c=PASSES_IN_BANK, u=2),
+                        )
+                    turned[s] = grouped
+                if s >= 1:
+                    nc.vector.quantize_mx(
+                        out=adj_codes[:, s - 1, :].bitcast(FP8X4),
+                        scales=adj_scales[:, s - 1, :],
+                        in_=turned[s - 1][:],
+                    )
+
+        with tc.tile_pool(name="tail", bufs=1) as tail:
+            deg = tail.tile([P, TILES], F32)
+            nc.vector.scalar_tensor_tensor(
+                out=deg[:], in0=sums_vector[:], scalar=1.0, in1=sums_scalar[:], op0=ALU.add, op1=ALU.add
+            )
+            root = tail.tile([P, TILES], F32)
+            nc.vector.tensor_scalar_max(out=root[:], in0=deg[:], scalar1=SMALLEST_DEG)
+            nc.scalar.activation(out=root[:], in_=root[:], func=ACT.Sqrt)
+            one_over_root = tail.tile([P, TILES], F32)
+            nc.vector.reciprocal(out=one_over_root[:], in_=root[:])
+            dinv = tail.tile([P, TILES], F32)
+            nc.vector.scalar_tensor_tensor(
+                out=dinv[:], in0=deg[:], scalar=0.0, in1=one_over_root[:], op0=ALU.is_gt, op1=ALU.mult
+            )
+            dinv_squared = tail.tile([P, TILES], F32)
+            nc.vector.tensor_mul(out=dinv_squared[:], in0=dinv[:], in1=dinv[:])
+
+            hs_grouped = tail.tile([P, PASSES, FEATS * PACK], BF16, align_bytes=64)
+            self_term = tail.tile([P, TILES * FEATS], F32)
+            for c in range(PASSES):
+                h_bank = psum.tile([P, BANK], F32, tag="bank")
+                for t in range(PACK):
+                    s = PACK * c + t
+                    h_tile = h_bank[:, t * FEATS : (t + 1) * FEATS]
+                    nc.tensor.matmul(h_tile, lhsT=ones[:], rhs=bias_rows[:], start=True, stop=False)
+                    nc.tensor.matmul(
+                        h_tile, lhsT=h_lnT[:, s * P : (s + 1) * P], rhs=w2_sb[:], start=False, stop=True
+                    )
+                nc.vector.tensor_tensor(
+                    out=hs_grouped[:, c, :].rearrange("q (f t) -> q f t", t=PACK),
+                    in0=h_bank[:].rearrange("q (t f) -> q f t", t=PACK),
+                    in1=dinv[:, PACK * c : PACK * (c + 1)].unsqueeze(1).to_broadcast([P, FEATS, PACK]),
+                    op=ALU.mult,
+                )
+                for t in range(PACK):
+                    s = PACK * c + t
+                    nc.scalar.activation(
+                        out=self_term[:, s * FEATS : (s + 1) * FEATS],
+                        in_=h_bank[:, t * FEATS : (t + 1) * FEATS],
+                        func=ACT.Copy,
+                        scale=dinv_squared[:, s : s + 1],
+                    )
+            hs_codes = tail.tile([P, PASSES * FEATS], U32, align_bytes=64)
+            hs_scales = tail.tile([P, PASSES * FEATS], U8, align_bytes=64)
+            nc.vector.quantize_mx(
+                out=hs_codes[:].bitcast(FP8X4),
+                scales=hs_scales[:],
+                in_=hs_grouped[:].rearrange("q c x -> q (c x)"),
+            )
+
+            for first in range(0, TILES, TILES_IN_BANK):
+                agg_bank = psum.tile([P, BANK], F32, tag="bank")
+                for place in range(TILES_IN_BANK):
+                    s = first + place
+                    for c in range(PASSES):
+                        nc.tensor.matmul_mx(
+                            out=agg_bank[:, place * FEATS : (place + 1) * FEATS],
+                            lhsT=adj_codes[:, s, c * P : (c + 1) * P].bitcast(FP8X4),
+                            lhsT_scale=adj_scales[:, s, c * P : (c + 1) * P],
+                            rhs=hs_codes[:, c * FEATS : (c + 1) * FEATS].bitcast(FP8X4),
+                            rhs_scale=hs_scales[:, c * FEATS : (c + 1) * FEATS],
+                            start=(c == 0),
+                            stop=(c == PASSES - 1),
+                        )
+                result = tail.tile([P, BANK], F32, tag="result", bufs=3)
+                for place in range(TILES_IN_BANK):
+                    s = first + place
+                    nc.vector.scalar_tensor_tensor(
+                        out=result[:, place * FEATS : (place + 1) * FEATS],
+                        in0=agg_bank[:, place * FEATS : (place + 1) * FEATS],
+                        scalar=dinv[:, s : s + 1],
+                        in1=self_term[:, s * FEATS : (s + 1) * FEATS],
+                        op0=ALU.mult,
+                        op1=ALU.add,
+                    )
+                nc.sync.dma_start(
+                    out=out_spans[:, first // 2 : (first + TILES_IN_BANK) // 2, :],
+                    in_=result[:].rearrange("p (g x) -> p g x", x=2 * FEATS),
+                )

@@ -22,8 +22,10 @@ BANKS_IN_TILE = PASSES // PASSES_IN_BANK
 TILES_IN_BANK = BANK // FEATS
 FEATURE_GROUP = 8
 
-SCALAR_SUM_COLS = 768
-VECTOR_SUM_COLS = NODES - SCALAR_SUM_COLS
+TENSOR_SUM_PASSES = 2
+TENSOR_SUM_COLS = TENSOR_SUM_PASSES * K_PASS
+ROWS_IN_CHUNK = P // PACK
+CHUNKS = P // ROWS_IN_CHUNK
 
 SMALLEST_DEG = 2.0**-100
 
@@ -49,6 +51,15 @@ def tile_gcnlayer_pb_t_kernel(tc, h_ln, adj, W2, b2, out):
         bias_rows = keep.tile([P, FEATS], BF16)
         nc.vector.memset(bias_rows[:], 0.0)
         nc.scalar.dma_start(out=bias_rows[0:1, :], in_=b2.rearrange("(o f) -> o f", o=1))
+        fold = keep.tile([P, CHUNKS, P], F32)
+        nc.vector.memset(fold[:], 0.0)
+        for chunk in range(CHUNKS):
+            nc.vector.tensor_reduce(
+                out=fold[:, chunk, chunk * ROWS_IN_CHUNK : (chunk + 1) * ROWS_IN_CHUNK],
+                in_=ident_f32[:].rearrange("k (i t) -> k i t", t=PACK),
+                axis=mybir.AxisListType.X,
+                op=ALU.add,
+            )
         table_warmer = keep.tile([P, 1], F32)
         nc.vector.memset(table_warmer[:], 1.0)
         nc.scalar.activation(out=table_warmer[:], in_=table_warmer[:], func=ACT.Sqrt)
@@ -57,11 +68,10 @@ def tile_gcnlayer_pb_t_kernel(tc, h_ln, adj, W2, b2, out):
         adj_scales = keep.tile([P, TILES, PASSES * P], U8, align_bytes=64)
         h_lnT = keep.tile([FEATS, NODES], BF16)
         sums_vector = keep.tile([P, TILES], F32)
-        sums_scalar = keep.tile([P, TILES], F32)
+        sums_tensor = psum.tile([P, CHUNKS * TILES], F32, tag="bank")
 
         with tc.tile_pool(name="stream", bufs=1) as stream:
-            unread_vector = stream.tile([P, VECTOR_SUM_COLS], BF16)
-            unread_scalar = stream.tile([P, SCALAR_SUM_COLS], BF16)
+            unread = stream.tile([P, NODES - TENSOR_SUM_COLS], BF16)
             turned = {}
             for s in range(TILES + 1):
                 if s < TILES:
@@ -69,19 +79,13 @@ def tile_gcnlayer_pb_t_kernel(tc, h_ln, adj, W2, b2, out):
                     nc.sync.dma_start(out=rows[:], in_=adj_tiles[:, s // 2, s % 2, :])
 
                     nc.vector.tensor_scalar(
-                        out=unread_vector[:],
-                        in0=rows[:, :VECTOR_SUM_COLS],
+                        out=unread[:],
+                        in0=rows[:, TENSOR_SUM_COLS:],
                         scalar1=1.0,
                         scalar2=None,
                         op0=ALU.mult,
                         op1=ALU.add,
                         accum_out=sums_vector[:, s : s + 1],
-                    )
-                    nc.scalar.activation(
-                        out=unread_scalar[:],
-                        in_=rows[:, VECTOR_SUM_COLS:],
-                        func=ACT.Copy,
-                        accum_out=sums_scalar[:, s : s + 1],
                     )
 
                     place = s % FEATURE_GROUP
@@ -123,6 +127,16 @@ def tile_gcnlayer_pb_t_kernel(tc, h_ln, adj, W2, b2, out):
                         )
                     turned[s] = grouped
                 if s >= 1:
+                    for chunk in range(CHUNKS):
+                        for c in range(TENSOR_SUM_PASSES):
+                            first_col = (c * P + chunk * ROWS_IN_CHUNK) * PACK
+                            nc.tensor.matmul(
+                                sums_tensor[:, chunk * TILES + s - 1 : chunk * TILES + s],
+                                lhsT=turned[s - 1][:, first_col : first_col + P],
+                                rhs=ones[:, 0:1],
+                                start=(c == 0),
+                                stop=(c == TENSOR_SUM_PASSES - 1),
+                            )
                     nc.vector.quantize_mx(
                         out=adj_codes[:, s - 1, :].bitcast(FP8X4),
                         scales=adj_scales[:, s - 1, :],
@@ -130,9 +144,21 @@ def tile_gcnlayer_pb_t_kernel(tc, h_ln, adj, W2, b2, out):
                     )
 
         with tc.tile_pool(name="tail", bufs=1) as tail:
+            sums_by_value = tail.tile([P, CHUNKS * TILES], F32)
+            nc.vector.tensor_copy(out=sums_by_value[:], in_=sums_tensor[:])
+            folded_bank = psum.tile([P, BANK], F32, tag="bank")
+            folded = folded_bank[:, :TILES]
+            for chunk in range(CHUNKS):
+                nc.tensor.matmul(
+                    folded,
+                    lhsT=fold[:, chunk, :],
+                    rhs=sums_by_value[:, chunk * TILES : (chunk + 1) * TILES],
+                    start=(chunk == 0),
+                    stop=(chunk == CHUNKS - 1),
+                )
             deg = tail.tile([P, TILES], F32)
             nc.vector.scalar_tensor_tensor(
-                out=deg[:], in0=sums_vector[:], scalar=1.0, in1=sums_scalar[:], op0=ALU.add, op1=ALU.add
+                out=deg[:], in0=folded, scalar=1.0, in1=sums_vector[:], op0=ALU.add, op1=ALU.add
             )
             root = tail.tile([P, TILES], F32)
             nc.vector.tensor_scalar_max(out=root[:], in0=deg[:], scalar1=SMALLEST_DEG)

@@ -22,7 +22,7 @@ BANKS_IN_TILE = PASSES // PASSES_IN_BANK
 TILES_IN_BANK = BANK // FEATS
 FEATURE_GROUP = 8
 
-TENSOR_SUM_PASSES = 2
+TENSOR_SUM_PASSES = 4
 TENSOR_SUM_COLS = TENSOR_SUM_PASSES * K_PASS
 ROWS_IN_CHUNK = P // PACK
 CHUNKS = P // ROWS_IN_CHUNK

@@ -19,13 +19,14 @@ PASSES = NODES // K_PASS
 BANK = 512
 PASSES_IN_BANK = BANK // (2 * P)
 BANKS_IN_TILE = PASSES // PASSES_IN_BANK
-TILES_IN_BANK = BANK // FEATS
 FEATURE_GROUP = 8
 
 TENSOR_SUM_PASSES = 4
 TENSOR_SUM_COLS = TENSOR_SUM_PASSES * K_PASS
 ROWS_IN_CHUNK = P // PACK
 CHUNKS = P // ROWS_IN_CHUNK
+
+EARLY_TILES = 4
 
 SMALLEST_DEG = 2.0**-100
 
@@ -66,7 +67,7 @@ def tile_gcnlayer_pb_t_kernel(tc, h_ln, adj, W2, b2, out):
 
         adj_codes = keep.tile([P, TILES, PASSES * P], U32, align_bytes=64)
         adj_scales = keep.tile([P, TILES, PASSES * P], U8, align_bytes=64)
-        h_lnT = keep.tile([FEATS, NODES], BF16)
+        features = keep.tile([P, TILES * FEATS], BF16)
         sums_vector = keep.tile([P, TILES], F32)
         sums_tensor = psum.tile([P, CHUNKS * TILES], F32, tag="bank")
 
@@ -77,6 +78,13 @@ def tile_gcnlayer_pb_t_kernel(tc, h_ln, adj, W2, b2, out):
                 if s < TILES:
                     rows = stream.tile([P, NODES], BF16, tag="rows", bufs=4)
                     nc.sync.dma_start(out=rows[:], in_=adj_tiles[:, s // 2, s % 2, :])
+                    if s % FEATURE_GROUP == 0:
+                        nc.sync.dma_start(
+                            out=features[:, s * FEATS : (s + FEATURE_GROUP) * FEATS].rearrange(
+                                "p (g x) -> p g x", x=2 * FEATS
+                            ),
+                            in_=h_ln_spans[:, s // 2 : (s + FEATURE_GROUP) // 2, :],
+                        )
 
                     nc.vector.tensor_scalar(
                         out=unread[:],
@@ -88,25 +96,24 @@ def tile_gcnlayer_pb_t_kernel(tc, h_ln, adj, W2, b2, out):
                         accum_out=sums_vector[:, s : s + 1],
                     )
 
-                    place = s % FEATURE_GROUP
-                    if place == 0:
-                        features = stream.tile([P, FEATURE_GROUP * FEATS], BF16, tag="features", bufs=2)
-                        first_span = s // 2
-                        nc.sync.dma_start(
-                            out=features[:].rearrange("p (g x) -> p g x", x=2 * FEATS),
-                            in_=h_ln_spans[:, first_span : first_span + FEATURE_GROUP // 2, :],
-                        )
-                        features_bank = psum.tile([FEATS, FEATURE_GROUP * P], BF16, tag="bank")
-                    nc.tensor.transpose(
-                        features_bank[:, place * P : (place + 1) * P],
-                        features[:, place * FEATS : (place + 1) * FEATS],
-                        ident_bf16[:],
+                if s >= 1:
+                    for chunk in range(CHUNKS):
+                        for c in range(TENSOR_SUM_PASSES):
+                            first_col = (c * P + chunk * ROWS_IN_CHUNK) * PACK
+                            nc.tensor.matmul(
+                                sums_tensor[:, chunk * TILES + s - 1 : chunk * TILES + s],
+                                lhsT=turned[s - 1][:, first_col : first_col + P],
+                                rhs=ones[:, 0:1],
+                                start=(c == 0),
+                                stop=(c == TENSOR_SUM_PASSES - 1),
+                            )
+                    nc.vector.quantize_mx(
+                        out=adj_codes[:, s - 1, :].bitcast(FP8X4),
+                        scales=adj_scales[:, s - 1, :],
+                        in_=turned[s - 1][:],
                     )
-                    if place == FEATURE_GROUP - 1:
-                        nc.scalar.copy(
-                            out=h_lnT[:, (s - place) * P : (s + 1) * P], in_=features_bank[:]
-                        )
 
+                if s < TILES:
                     row_words = rows[:].bitcast(F32)
                     grouped = stream.tile([P, NODES], BF16, tag="grouped", bufs=2, align_bytes=64)
                     grouped_words = grouped[:].bitcast(F32).rearrange(
@@ -126,24 +133,22 @@ def tile_gcnlayer_pb_t_kernel(tc, h_ln, adj, W2, b2, out):
                             in_=bank[:].rearrange("q (c u i) -> q c i u", c=PASSES_IN_BANK, u=2),
                         )
                     turned[s] = grouped
-                if s >= 1:
-                    for chunk in range(CHUNKS):
-                        for c in range(TENSOR_SUM_PASSES):
-                            first_col = (c * P + chunk * ROWS_IN_CHUNK) * PACK
-                            nc.tensor.matmul(
-                                sums_tensor[:, chunk * TILES + s - 1 : chunk * TILES + s],
-                                lhsT=turned[s - 1][:, first_col : first_col + P],
-                                rhs=ones[:, 0:1],
-                                start=(c == 0),
-                                stop=(c == TENSOR_SUM_PASSES - 1),
-                            )
-                    nc.vector.quantize_mx(
-                        out=adj_codes[:, s - 1, :].bitcast(FP8X4),
-                        scales=adj_scales[:, s - 1, :],
-                        in_=turned[s - 1][:],
-                    )
 
         with tc.tile_pool(name="tail", bufs=1) as tail:
+            h_lnT = tail.tile([FEATS, NODES], BF16)
+            for first in range(0, TILES, FEATURE_GROUP):
+                features_bank = psum.tile([FEATS, FEATURE_GROUP * P], BF16, tag="bank")
+                for place in range(FEATURE_GROUP):
+                    s = first + place
+                    nc.tensor.transpose(
+                        features_bank[:, place * P : (place + 1) * P],
+                        features[:, s * FEATS : (s + 1) * FEATS],
+                        ident_bf16[:],
+                    )
+                nc.scalar.copy(
+                    out=h_lnT[:, first * P : (first + FEATURE_GROUP) * P], in_=features_bank[:]
+                )
+
             sums_by_value = tail.tile([P, CHUNKS * TILES], F32)
             nc.vector.tensor_copy(out=sums_by_value[:], in_=sums_tensor[:])
             folded_bank = psum.tile([P, BANK], F32, tag="bank")
@@ -173,15 +178,18 @@ def tile_gcnlayer_pb_t_kernel(tc, h_ln, adj, W2, b2, out):
             nc.vector.tensor_mul(out=dinv_squared[:], in0=dinv[:], in1=dinv[:])
 
             hs_grouped = tail.tile([P, PASSES, FEATS * PACK], BF16, align_bytes=64)
-            self_term = tail.tile([P, TILES * FEATS], F32)
-            for c in range(PASSES):
+            hs_codes = tail.tile([P, PASSES, FEATS], U32, align_bytes=64)
+            hs_scales = tail.tile([P, PASSES, FEATS], U8, align_bytes=64)
+            self_term = tail.tile([P, TILES, FEATS], F32)
+
+            def make_hs(c):
                 h_bank = psum.tile([P, BANK], F32, tag="bank")
                 for t in range(PACK):
-                    s = PACK * c + t
                     h_tile = h_bank[:, t * FEATS : (t + 1) * FEATS]
+                    first_node = (PACK * c + t) * P
                     nc.tensor.matmul(h_tile, lhsT=ones[:], rhs=bias_rows[:], start=True, stop=False)
                     nc.tensor.matmul(
-                        h_tile, lhsT=h_lnT[:, s * P : (s + 1) * P], rhs=w2_sb[:], start=False, stop=True
+                        h_tile, lhsT=h_lnT[:, first_node : first_node + P], rhs=w2_sb[:], start=False, stop=True
                     )
                 nc.vector.tensor_tensor(
                     out=hs_grouped[:, c, :].rearrange("q (f t) -> q f t", t=PACK),
@@ -190,47 +198,53 @@ def tile_gcnlayer_pb_t_kernel(tc, h_ln, adj, W2, b2, out):
                     op=ALU.mult,
                 )
                 for t in range(PACK):
-                    s = PACK * c + t
                     nc.scalar.activation(
-                        out=self_term[:, s * FEATS : (s + 1) * FEATS],
+                        out=self_term[:, PACK * c + t, :],
                         in_=h_bank[:, t * FEATS : (t + 1) * FEATS],
                         func=ACT.Copy,
-                        scale=dinv_squared[:, s : s + 1],
+                        scale=dinv_squared[:, PACK * c + t : PACK * c + t + 1],
                     )
-            hs_codes = tail.tile([P, PASSES * FEATS], U32, align_bytes=64)
-            hs_scales = tail.tile([P, PASSES * FEATS], U8, align_bytes=64)
-            nc.vector.quantize_mx(
-                out=hs_codes[:].bitcast(FP8X4),
-                scales=hs_scales[:],
-                in_=hs_grouped[:].rearrange("q c x -> q (c x)"),
-            )
 
-            for first in range(0, TILES, TILES_IN_BANK):
-                agg_bank = psum.tile([P, BANK], F32, tag="bank")
-                for place in range(TILES_IN_BANK):
-                    s = first + place
-                    for c in range(PASSES):
-                        nc.tensor.matmul_mx(
-                            out=agg_bank[:, place * FEATS : (place + 1) * FEATS],
-                            lhsT=adj_codes[:, s, c * P : (c + 1) * P].bitcast(FP8X4),
-                            lhsT_scale=adj_scales[:, s, c * P : (c + 1) * P],
-                            rhs=hs_codes[:, c * FEATS : (c + 1) * FEATS].bitcast(FP8X4),
-                            rhs_scale=hs_scales[:, c * FEATS : (c + 1) * FEATS],
-                            start=(c == 0),
-                            stop=(c == PASSES - 1),
-                        )
-                result = tail.tile([P, BANK], F32, tag="result", bufs=3)
-                for place in range(TILES_IN_BANK):
-                    s = first + place
-                    nc.vector.scalar_tensor_tensor(
-                        out=result[:, place * FEATS : (place + 1) * FEATS],
-                        in0=agg_bank[:, place * FEATS : (place + 1) * FEATS],
-                        scalar=dinv[:, s : s + 1],
-                        in1=self_term[:, s * FEATS : (s + 1) * FEATS],
-                        op0=ALU.mult,
-                        op1=ALU.add,
-                    )
-                nc.sync.dma_start(
-                    out=out_spans[:, first // 2 : (first + TILES_IN_BANK) // 2, :],
-                    in_=result[:].rearrange("p (g x) -> p g x", x=2 * FEATS),
+            def run_pass(agg, s, c):
+                nc.tensor.matmul_mx(
+                    out=agg,
+                    lhsT=adj_codes[:, s, c * P : (c + 1) * P].bitcast(FP8X4),
+                    lhsT_scale=adj_scales[:, s, c * P : (c + 1) * P],
+                    rhs=hs_codes[:, c, :].bitcast(FP8X4),
+                    rhs_scale=hs_scales[:, c, :],
+                    start=(c == 0),
+                    stop=(c == PASSES - 1),
                 )
+
+            aggs = {}
+            for s in range(EARLY_TILES):
+                aggs[s] = psum.tile([P, FEATS], F32, tag="bank", name="early_agg_%d" % s)
+            for c in range(PASSES + 1):
+                if c < PASSES:
+                    make_hs(c)
+                if c >= 1:
+                    nc.vector.quantize_mx(
+                        out=hs_codes[:, c - 1, :].bitcast(FP8X4),
+                        scales=hs_scales[:, c - 1, :],
+                        in_=hs_grouped[:, c - 1, :],
+                    )
+                    for s in range(EARLY_TILES):
+                        run_pass(aggs[s][:], s, c - 1)
+
+            for s in range(TILES):
+                if s >= EARLY_TILES:
+                    aggs[s] = psum.tile([P, FEATS], F32, tag="bank", name="agg")
+                    for c in range(PASSES):
+                        run_pass(aggs[s][:], s, c)
+                if s % 2 == 0:
+                    result = tail.tile([P, 2 * FEATS], F32, tag="result", bufs=4)
+                nc.vector.scalar_tensor_tensor(
+                    out=result[:, (s % 2) * FEATS : (s % 2 + 1) * FEATS],
+                    in0=aggs[s][:],
+                    scalar=dinv[:, s : s + 1],
+                    in1=self_term[:, s, :],
+                    op0=ALU.mult,
+                    op1=ALU.add,
+                )
+                if s % 2 == 1:
+                    nc.sync.dma_start(out=out_spans[:, s // 2, :], in_=result[:])

@@ -20,6 +20,7 @@ BANK = 512
 PASSES_IN_BANK = BANK // (2 * P)
 BANKS_IN_TILE = PASSES // PASSES_IN_BANK
 FEATURE_GROUP = 8
+PASSES_IN_GROUP = FEATURE_GROUP // PACK
 
 TENSOR_SUM_PASSES = 4
 TENSOR_SUM_COLS = TENSOR_SUM_PASSES * K_PASS
@@ -77,7 +78,8 @@ def tile_gcnlayer_pb_t_kernel(tc, h_ln, adj, W2, b2, out):
             for s in range(TILES + 1):
                 if s < TILES:
                     rows = stream.tile([P, NODES], BF16, tag="rows", bufs=4)
-                    nc.sync.dma_start(out=rows[:], in_=adj_tiles[:, s // 2, s % 2, :])
+                    for cols in (slice(0, NODES // 2), slice(NODES // 2, NODES)):
+                        nc.sync.dma_start(out=rows[:, cols], in_=adj_tiles[:, s // 2, s % 2, cols])
                     if s % FEATURE_GROUP == 0:
                         nc.sync.dma_start(
                             out=features[:, s * FEATS : (s + FEATURE_GROUP) * FEATS].rearrange(
@@ -96,24 +98,6 @@ def tile_gcnlayer_pb_t_kernel(tc, h_ln, adj, W2, b2, out):
                         accum_out=sums_vector[:, s : s + 1],
                     )
 
-                if s >= 1:
-                    for chunk in range(CHUNKS):
-                        for c in range(TENSOR_SUM_PASSES):
-                            first_col = (c * P + chunk * ROWS_IN_CHUNK) * PACK
-                            nc.tensor.matmul(
-                                sums_tensor[:, chunk * TILES + s - 1 : chunk * TILES + s],
-                                lhsT=turned[s - 1][:, first_col : first_col + P],
-                                rhs=ones[:, 0:1],
-                                start=(c == 0),
-                                stop=(c == TENSOR_SUM_PASSES - 1),
-                            )
-                    nc.vector.quantize_mx(
-                        out=adj_codes[:, s - 1, :].bitcast(FP8X4),
-                        scales=adj_scales[:, s - 1, :],
-                        in_=turned[s - 1][:],
-                    )
-
-                if s < TILES:
                     row_words = rows[:].bitcast(F32)
                     grouped = stream.tile([P, NODES], BF16, tag="grouped", bufs=2, align_bytes=64)
                     grouped_words = grouped[:].bitcast(F32).rearrange(
@@ -134,20 +118,40 @@ def tile_gcnlayer_pb_t_kernel(tc, h_ln, adj, W2, b2, out):
                         )
                     turned[s] = grouped
 
+                if s >= 1:
+                    for chunk in range(CHUNKS):
+                        for c in range(TENSOR_SUM_PASSES):
+                            first_col = (c * P + chunk * ROWS_IN_CHUNK) * PACK
+                            nc.tensor.matmul(
+                                sums_tensor[:, chunk * TILES + s - 1 : chunk * TILES + s],
+                                lhsT=turned[s - 1][:, first_col : first_col + P],
+                                rhs=ones[:, 0:1],
+                                start=(c == 0),
+                                stop=(c == TENSOR_SUM_PASSES - 1),
+                            )
+                    nc.vector.quantize_mx(
+                        out=adj_codes[:, s - 1, :].bitcast(FP8X4),
+                        scales=adj_scales[:, s - 1, :],
+                        in_=turned[s - 1][:],
+                    )
+
         with tc.tile_pool(name="tail", bufs=1) as tail:
             h_lnT = tail.tile([FEATS, NODES], BF16)
-            for first in range(0, TILES, FEATURE_GROUP):
+
+            def turn_features(group):
+                first = group * FEATURE_GROUP
                 features_bank = psum.tile([FEATS, FEATURE_GROUP * P], BF16, tag="bank")
                 for place in range(FEATURE_GROUP):
-                    s = first + place
                     nc.tensor.transpose(
                         features_bank[:, place * P : (place + 1) * P],
-                        features[:, s * FEATS : (s + 1) * FEATS],
+                        features[:, (first + place) * FEATS : (first + place + 1) * FEATS],
                         ident_bf16[:],
                     )
                 nc.scalar.copy(
                     out=h_lnT[:, first * P : (first + FEATURE_GROUP) * P], in_=features_bank[:]
                 )
+
+            turn_features(0)
 
             sums_by_value = tail.tile([P, CHUNKS * TILES], F32)
             nc.vector.tensor_copy(out=sums_by_value[:], in_=sums_tensor[:])
@@ -222,6 +226,8 @@ def tile_gcnlayer_pb_t_kernel(tc, h_ln, adj, W2, b2, out):
             for c in range(PASSES + 1):
                 if c < PASSES:
                     make_hs(c)
+                    if c % PASSES_IN_GROUP == 0 and c + PASSES_IN_GROUP < PASSES:
+                        turn_features(c // PASSES_IN_GROUP + 1)
                 if c >= 1:
                     nc.vector.quantize_mx(
                         out=hs_codes[:, c - 1, :].bitcast(FP8X4),

import concourse.mybir as mybir
from concourse.masks import make_identity

F32 = mybir.dt.float32
BF16 = mybir.dt.bfloat16
U32 = mybir.dt.uint32
U8 = mybir.dt.uint8
FP8X4 = mybir.dt.float8_e4m3fn_x4
ALU = mybir.AluOpType
ACT = mybir.ActivationFunctionType

P = 128
NODES = 4096
FEATS = 128
TILES = NODES // P
PACK = 4
K_PASS = P * PACK
PASSES = NODES // K_PASS
BANK = 512
PASSES_IN_BANK = BANK // (2 * P)
BANKS_IN_TILE = PASSES // PASSES_IN_BANK
FEATURE_GROUP = 8
PASSES_IN_GROUP = FEATURE_GROUP // PACK

TENSOR_SUM_PASSES = 4
TENSOR_SUM_COLS = TENSOR_SUM_PASSES * K_PASS
ROWS_IN_CHUNK = P // PACK
CHUNKS = P // ROWS_IN_CHUNK

EARLY_TILES = 4

SMALLEST_DEG = 2.0**-100

FLOPS = 2 * NODES * NODES * FEATS + 2 * NODES * FEATS * FEATS


def tile_gcnlayer_pb_t_kernel(tc, h_ln, adj, W2, b2, out):
    nc = tc.nc

    adj_tiles = adj.rearrange("(g p e) j -> p g e j", p=P, e=2)
    h_ln_spans = h_ln.rearrange("(g p e) k -> p g (e k)", p=P, e=2)
    out_spans = out.rearrange("(g p e) f -> p g (e f)", p=P, e=2)

    with tc.tile_pool(name="keep", bufs=1) as keep, tc.psum_pool(name="psum", bufs=8) as psum:
        ident_f32 = keep.tile([P, P], F32)
        make_identity(nc, ident_f32[:])
        ident_bf16 = keep.tile([P, P], BF16)
        make_identity(nc, ident_bf16[:])
        w2_sb = keep.tile([FEATS, FEATS], BF16)
        nc.scalar.dma_start(out=w2_sb[:], in_=W2)
        ones = keep.tile([P, P], BF16)
        nc.vector.memset(ones[:], 1.0)
        bias_rows = keep.tile([P, FEATS], BF16)
        nc.vector.memset(bias_rows[:], 0.0)
        nc.scalar.dma_start(out=bias_rows[0:1, :], in_=b2.rearrange("(o f) -> o f", o=1))
        fold = keep.tile([P, CHUNKS, P], F32)
        nc.vector.memset(fold[:], 0.0)
        for chunk in range(CHUNKS):
            nc.vector.tensor_reduce(
                out=fold[:, chunk, chunk * ROWS_IN_CHUNK : (chunk + 1) * ROWS_IN_CHUNK],
                in_=ident_f32[:].rearrange("k (i t) -> k i t", t=PACK),
                axis=mybir.AxisListType.X,
                op=ALU.add,
            )
        table_warmer = keep.tile([P, 1], F32)
        nc.vector.memset(table_warmer[:], 1.0)
        nc.scalar.activation(out=table_warmer[:], in_=table_warmer[:], func=ACT.Sqrt)

        adj_codes = keep.tile([P, TILES, PASSES * P], U32, align_bytes=64)
        adj_scales = keep.tile([P, TILES, PASSES * P], U8, align_bytes=64)
        features = keep.tile([P, TILES * FEATS], BF16)
        sums_vector = keep.tile([P, TILES], F32)
        sums_tensor = psum.tile([P, CHUNKS * TILES], F32, tag="bank")

        with tc.tile_pool(name="stream", bufs=1) as stream:
            unread = stream.tile([P, NODES - TENSOR_SUM_COLS], BF16)
            turned = {}
            for s in range(TILES + 1):
                if s < TILES:
                    rows = stream.tile([P, NODES], BF16, tag="rows", bufs=4)
                    for cols in (slice(0, NODES // 2), slice(NODES // 2, NODES)):
                        nc.sync.dma_start(out=rows[:, cols], in_=adj_tiles[:, s // 2, s % 2, cols])
                    if s % FEATURE_GROUP == 0:
                        nc.sync.dma_start(
                            out=features[:, s * FEATS : (s + FEATURE_GROUP) * FEATS].rearrange(
                                "p (g x) -> p g x", x=2 * FEATS
                            ),
                            in_=h_ln_spans[:, s // 2 : (s + FEATURE_GROUP) // 2, :],
                        )

                    nc.vector.tensor_scalar(
                        out=unread[:],
                        in0=rows[:, TENSOR_SUM_COLS:],
                        scalar1=1.0,
                        scalar2=None,
                        op0=ALU.mult,
                        op1=ALU.add,
                        accum_out=sums_vector[:, s : s + 1],
                    )

                    row_words = rows[:].bitcast(F32)
                    grouped = stream.tile([P, NODES], BF16, tag="grouped", bufs=2, align_bytes=64)
                    grouped_words = grouped[:].bitcast(F32).rearrange(
                        "q (c i u) -> q c i u", c=PASSES, u=2
                    )
                    for b in range(BANKS_IN_TILE):
                        bank = psum.tile([P, BANK], F32, tag="bank")
                        for half in range(2 * PASSES_IN_BANK):
                            block = 2 * PASSES_IN_BANK * b + half
                            nc.tensor.transpose(
                                bank[:, half * P : (half + 1) * P],
                                row_words[:, block * P : (block + 1) * P],
                                ident_f32[:],
                            )
                        nc.scalar.copy(
                            out=grouped_words[:, b * PASSES_IN_BANK : (b + 1) * PASSES_IN_BANK, :, :],
                            in_=bank[:].rearrange("q (c u i) -> q c i u", c=PASSES_IN_BANK, u=2),
                        )
                    turned[s] = grouped

                if s >= 1:
                    for chunk in range(CHUNKS):
                        for c in range(TENSOR_SUM_PASSES):
                            first_col = (c * P + chunk * ROWS_IN_CHUNK) * PACK
                            nc.tensor.matmul(
                                sums_tensor[:, chunk * TILES + s - 1 : chunk * TILES + s],
                                lhsT=turned[s - 1][:, first_col : first_col + P],
                                rhs=ones[:, 0:1],
                                start=(c == 0),
                                stop=(c == TENSOR_SUM_PASSES - 1),
                            )
                    nc.vector.quantize_mx(
                        out=adj_codes[:, s - 1, :].bitcast(FP8X4),
                        scales=adj_scales[:, s - 1, :],
                        in_=turned[s - 1][:],
                    )

        with tc.tile_pool(name="tail", bufs=1) as tail:
            h_lnT = tail.tile([FEATS, NODES], BF16)

            def turn_features(group):
                first = group * FEATURE_GROUP
                features_bank = psum.tile([FEATS, FEATURE_GROUP * P], BF16, tag="bank")
                for place in range(FEATURE_GROUP):
                    nc.tensor.transpose(
                        features_bank[:, place * P : (place + 1) * P],
                        features[:, (first + place) * FEATS : (first + place + 1) * FEATS],
                        ident_bf16[:],
                    )
                nc.scalar.copy(
                    out=h_lnT[:, first * P : (first + FEATURE_GROUP) * P], in_=features_bank[:]
                )

            turn_features(0)

            sums_by_value = tail.tile([P, CHUNKS * TILES], F32)
            nc.vector.tensor_copy(out=sums_by_value[:], in_=sums_tensor[:])
            folded_bank = psum.tile([P, BANK], F32, tag="bank")
            folded = folded_bank[:, :TILES]
            for chunk in range(CHUNKS):
                nc.tensor.matmul(
                    folded,
                    lhsT=fold[:, chunk, :],
                    rhs=sums_by_value[:, chunk * TILES : (chunk + 1) * TILES],
                    start=(chunk == 0),
                    stop=(chunk == CHUNKS - 1),
                )
            deg = tail.tile([P, TILES], F32)
            nc.vector.scalar_tensor_tensor(
                out=deg[:], in0=folded, scalar=1.0, in1=sums_vector[:], op0=ALU.add, op1=ALU.add
            )
            root = tail.tile([P, TILES], F32)
            nc.vector.tensor_scalar_max(out=root[:], in0=deg[:], scalar1=SMALLEST_DEG)
            nc.scalar.activation(out=root[:], in_=root[:], func=ACT.Sqrt)
            one_over_root = tail.tile([P, TILES], F32)
            nc.vector.reciprocal(out=one_over_root[:], in_=root[:])
            dinv = tail.tile([P, TILES], F32)
            nc.vector.scalar_tensor_tensor(
                out=dinv[:], in0=deg[:], scalar=0.0, in1=one_over_root[:], op0=ALU.is_gt, op1=ALU.mult
            )
            dinv_squared = tail.tile([P, TILES], F32)
            nc.vector.tensor_mul(out=dinv_squared[:], in0=dinv[:], in1=dinv[:])

            hs_grouped = tail.tile([P, PASSES, FEATS * PACK], BF16, align_bytes=64)
            hs_codes = tail.tile([P, PASSES, FEATS], U32, align_bytes=64)
            hs_scales = tail.tile([P, PASSES, FEATS], U8, align_bytes=64)
            self_term = tail.tile([P, TILES, FEATS], F32)

            def make_hs(c):
                h_bank = psum.tile([P, BANK], F32, tag="bank")
                for t in range(PACK):
                    h_tile = h_bank[:, t * FEATS : (t + 1) * FEATS]
                    first_node = (PACK * c + t) * P
                    nc.tensor.matmul(h_tile, lhsT=ones[:], rhs=bias_rows[:], start=True, stop=False)
                    nc.tensor.matmul(
                        h_tile, lhsT=h_lnT[:, first_node : first_node + P], rhs=w2_sb[:], start=False, stop=True
                    )
                nc.vector.tensor_tensor(
                    out=hs_grouped[:, c, :].rearrange("q (f t) -> q f t", t=PACK),
                    in0=h_bank[:].rearrange("q (t f) -> q f t", t=PACK),
                    in1=dinv[:, PACK * c : PACK * (c + 1)].unsqueeze(1).to_broadcast([P, FEATS, PACK]),
                    op=ALU.mult,
                )
                for t in range(PACK):
                    nc.scalar.activation(
                        out=self_term[:, PACK * c + t, :],
                        in_=h_bank[:, t * FEATS : (t + 1) * FEATS],
                        func=ACT.Copy,
                        scale=dinv_squared[:, PACK * c + t : PACK * c + t + 1],
                    )

            def run_pass(agg, s, c):
                nc.tensor.matmul_mx(
                    out=agg,
                    lhsT=adj_codes[:, s, c * P : (c + 1) * P].bitcast(FP8X4),
                    lhsT_scale=adj_scales[:, s, c * P : (c + 1) * P],
                    rhs=hs_codes[:, c, :].bitcast(FP8X4),
                    rhs_scale=hs_scales[:, c, :],
                    start=(c == 0),
                    stop=(c == PASSES - 1),
                )

            aggs = {}
            for s in range(EARLY_TILES):
                aggs[s] = psum.tile([P, FEATS], F32, tag="bank", name="early_agg_%d" % s)
            for c in range(PASSES + 1):
                if c < PASSES:
                    make_hs(c)
                    if c % PASSES_IN_GROUP == 0 and c + PASSES_IN_GROUP < PASSES:
                        turn_features(c // PASSES_IN_GROUP + 1)
                if c >= 1:
                    nc.vector.quantize_mx(
                        out=hs_codes[:, c - 1, :].bitcast(FP8X4),
                        scales=hs_scales[:, c - 1, :],
                        in_=hs_grouped[:, c - 1, :],
                    )
                    for s in range(EARLY_TILES):
                        run_pass(aggs[s][:], s, c - 1)

            for s in range(TILES):
                if s >= EARLY_TILES:
                    aggs[s] = psum.tile([P, FEATS], F32, tag="bank", name="agg")
                    for c in range(PASSES):
                        run_pass(aggs[s][:], s, c)
                if s % 2 == 0:
                    result = tail.tile([P, 2 * FEATS], F32, tag="result", bufs=4)
                nc.vector.scalar_tensor_tensor(
                    out=result[:, (s % 2) * FEATS : (s % 2 + 1) * FEATS],
                    in0=aggs[s][:],
                    scalar=dinv[:, s : s + 1],
                    in1=self_term[:, s, :],
                    op0=ALU.mult,
                    op1=ALU.add,
                )
                if s % 2 == 1:
                    nc.sync.dma_start(out=out_spans[:, s // 2, :], in_=result[:])
